import numpy as np
import ml_dtypes

BF16 = ml_dtypes.bfloat16


def bf(x):
    return np.asarray(x, np.float32).astype(BF16)


def f32(x):
    return np.asarray(x, np.float32)


def f64(x):
    return np.asarray(x).astype(np.float64)


def striped(idx):
    return np.tile(idx.reshape(-1, 16).T, (8, 1))


D, M, R, S, N = 128, 128, 128, 1024, 256
IMG_SCALE, AI_SCALE, ATT_NORM = 16.0, 1.5, 4.0


def setup_inputs():
    return {"table": bf(np.random.standard_normal((D, S))), "w_aw": bf(np.random.standard_normal((D, M)) / np.sqrt(D)), "b_aw": f32(0.1 * np.random.standard_normal((M, 1))), "img": bf(IMG_SCALE * np.maximum(np.random.standard_normal((D, R)), 0.0)), "w_ai": bf(AI_SCALE * np.random.standard_normal((D, M)) / (IMG_SCALE * np.sqrt(D))), "w_att": bf(ATT_NORM * np.random.standard_normal((M, 1)) / np.sqrt(M)), "offs": striped(np.random.permutation(np.tile(np.arange(S), 2))[:N])}


def reference(table, w_aw, b_aw, img, w_ai, w_att, offs):
    idx = offs[:16].T.reshape(-1)
    aw = f64(w_aw).T @ f64(table)[:, idx] + f64(b_aw)
    ai = f64(w_ai).T @ f64(img)
    score = (f64(w_att)[:, :, None] * np.tanh(ai[:, :, None] + aw[:, None, :])).sum(axis=0)
    p = np.exp(score - score.max(axis=0, keepdims=True))
    p = p / p.sum(axis=0, keepdims=True)
    return f64(img) @ p / R

@@ -1,0 +1,92 @@
+import concourse.mybir as mybir
+from concourse.masks import make_identity
+
+P = 128
+S = 1024
+N = 256
+BLOCKS = N // P
+
+FLOPS = 2 * P * P * (N + P + N + N)
+BYTES = 2 * P * N + 3 * 2 * P * P + 4 * P + 2 * P + 2 * P * (N // 16) + 4 * P * N
+
+BF16, F32, U16 = mybir.dt.bfloat16, mybir.dt.float32, mybir.dt.uint16
+TANH, EXP = mybir.ActivationFunctionType.Tanh, mybir.ActivationFunctionType.Exp
+MULT = mybir.AluOpType.mult
+ALONG_ROW = mybir.AxisListType.X
+
+
+def tile_imgwordatt_kernel(tc, table, w_aw, b_aw, img, w_ai, w_att, offs, out):
+    nc = tc.nc
+    with (
+        tc.tile_pool(name="held", bufs=1) as held,
+        tc.tile_pool(name="tanh_ring", bufs=4) as tanh_ring,
+        tc.psum_pool(name="score_banks", bufs=1) as score_banks,
+    ):
+        offsets = held.tile([P, N // 16], U16, name="offsets")
+        nc.sync.dma_start(offsets[:], offs)
+        table_sb = held.tile([P, S], BF16, name="table_sb")
+        nc.sync.dma_start(table_sb[:], table)
+        w_aw_sb = held.tile([P, P], BF16, name="w_aw_sb")
+        nc.scalar.dma_start(w_aw_sb[:], w_aw)
+        img_sb = held.tile([P, P], BF16, name="img_sb")
+        nc.scalar.dma_start(img_sb[:], img)
+        w_ai_sb = held.tile([P, P], BF16, name="w_ai_sb")
+        nc.gpsimd.dma_start(w_ai_sb[:], w_ai)
+        b_aw_sb = held.tile([P, 1], F32, name="b_aw_sb")
+        nc.gpsimd.dma_start(b_aw_sb[:], b_aw)
+        w_att_sb = held.tile([P, 1], BF16, name="w_att_sb")
+        nc.gpsimd.dma_start(w_att_sb[:], w_att)
+
+        identity = held.tile([P, P], BF16, name="identity")
+        make_identity(nc, identity[:])
+
+        aw_sb = held.tile([P, N], F32, name="aw_sb")
+        ai_sb = held.tile([P, P], F32, name="ai_sb")
+        imgT_sb = held.tile([P, P], BF16, name="imgT_sb")
+        with tc.psum_pool(name="head_banks", bufs=1) as head_banks:
+            aw_ps = head_banks.tile([P, N], F32, name="aw_ps")
+            nc.tensor.matmul(aw_ps[:], w_aw_sb[:], table_sb[:].indirect(offsets[:]), start=True, stop=True)
+            nc.vector.tensor_copy(aw_sb[:], aw_ps[:])
+
+            ai_ps = head_banks.tile([P, P], F32, name="ai_ps")
+            nc.tensor.matmul(ai_ps[:], w_ai_sb[:], img_sb[:], start=True, stop=True)
+            nc.vector.tensor_scalar_add(ai_sb[:], ai_ps[:], b_aw_sb[:, 0:1])
+
+            imgT_ps = head_banks.tile([P, P], BF16, name="imgT_ps")
+            nc.tensor.transpose(imgT_ps[:], img_sb[:], identity[:])
+            nc.vector.tensor_copy(imgT_sb[:], imgT_ps[:])
+
+        scoreT = [score_banks.tile([P, P], F32, name=f"scoreT{b}") for b in range(BLOCKS)]
+        for r in range(P):
+            tanh_r = tanh_ring.tile([P, N], BF16, name="tanh_r")
+            nc.scalar.activation(tanh_r[:], aw_sb[:], TANH, bias=ai_sb[:, r : r + 1])
+            for b in range(BLOCKS):
+                nc.tensor.matmul(
+                    scoreT[b][:, r : r + 1], tanh_r[:, b * P : (b + 1) * P], w_att_sb[:, 0:1], start=True, stop=True
+                )
+
+        with (
+            tc.tile_pool(name="tail", bufs=BLOCKS) as tail,
+            tc.psum_pool(name="tail_banks", bufs=BLOCKS) as tail_banks,
+        ):
+            for b in range(BLOCKS):
+                neg_max = tail.tile([P, 1], F32, name="neg_max")
+                nc.vector.reduce_max(neg_max[:], scoreT[b][:], ALONG_ROW, negate=True)
+                expT = tail.tile([P, P], F32, name="expT")
+                exp_sum = tail.tile([P, 1], F32, name="exp_sum")
+                nc.scalar.activation(expT[:], scoreT[b][:], EXP, bias=neg_max[:, 0:1], accum_out=exp_sum[:, 0:1])
+                inv_sum = tail.tile([P, 1], F32, name="inv_sum")
+                nc.vector.reciprocal(inv_sum[:], exp_sum[:])
+                pT = tail.tile([P, P], BF16, name="pT")
+                nc.vector.tensor_scalar(pT[:], expT[:], inv_sum[:, 0:1], 1.0 / P, MULT, MULT)
+
+                p_ps = tail_banks.tile([P, P], BF16, name="p_ps")
+                nc.tensor.transpose(p_ps[:], pT[:], identity[:])
+                p_sb = tail.tile([P, P], BF16, name="p_sb")
+                nc.vector.tensor_copy(p_sb[:], p_ps[:])
+
+                out_ps = tail_banks.tile([P, P], F32, name="out_ps")
+                nc.tensor.matmul(out_ps[:], imgT_sb[:], p_sb[:], start=True, stop=True)
+                out_sb = tail.tile([P, P], F32, name="out_sb")
+                nc.vector.tensor_copy(out_sb[:], out_ps[:])
+                nc.sync.dma_start(out[:, b * P : (b + 1) * P], out_sb[:])

@@ -11,7 +11,6 @@ BYTES = 2 * P * N + 3 * 2 * P * P + 4 * P + 2 * P + 2 * P * (N // 16) + 4 * P * 
 
 BF16, F32, U16 = mybir.dt.bfloat16, mybir.dt.float32, mybir.dt.uint16
 TANH, EXP = mybir.ActivationFunctionType.Tanh, mybir.ActivationFunctionType.Exp
-MULT = mybir.AluOpType.mult
 ALONG_ROW = mybir.AxisListType.X
 
 
@@ -25,17 +24,18 @@ def tile_imgwordatt_kernel(tc, table, w_aw, b_aw, img, w_ai, w_att, offs, out):
         offsets = held.tile([P, N // 16], U16, name="offsets")
         nc.sync.dma_start(offsets[:], offs)
         table_sb = held.tile([P, S], BF16, name="table_sb")
-        nc.sync.dma_start(table_sb[:], table)
+        nc.sync.dma_start(table_sb[:, : S // 2], table[:, : S // 2])
+        nc.scalar.dma_start(table_sb[:, S // 2 :], table[:, S // 2 :])
         w_aw_sb = held.tile([P, P], BF16, name="w_aw_sb")
-        nc.scalar.dma_start(w_aw_sb[:], w_aw)
+        nc.sync.dma_start(w_aw_sb[:], w_aw)
         img_sb = held.tile([P, P], BF16, name="img_sb")
         nc.scalar.dma_start(img_sb[:], img)
         w_ai_sb = held.tile([P, P], BF16, name="w_ai_sb")
-        nc.gpsimd.dma_start(w_ai_sb[:], w_ai)
+        nc.scalar.dma_start(w_ai_sb[:], w_ai)
         b_aw_sb = held.tile([P, 1], F32, name="b_aw_sb")
-        nc.gpsimd.dma_start(b_aw_sb[:], b_aw)
+        nc.sync.dma_start(b_aw_sb[:], b_aw)
         w_att_sb = held.tile([P, 1], BF16, name="w_att_sb")
-        nc.gpsimd.dma_start(w_att_sb[:], w_att)
+        nc.scalar.dma_start(w_att_sb[:], w_att)
 
         identity = held.tile([P, P], BF16, name="identity")
         make_identity(nc, identity[:])
@@ -65,28 +65,39 @@ def tile_imgwordatt_kernel(tc, table, w_aw, b_aw, img, w_ai, w_att, offs, out):
                     scoreT[b][:, r : r + 1], tanh_r[:, b * P : (b + 1) * P], w_att_sb[:, 0:1], start=True, stop=True
                 )
 
+        blocks = range(BLOCKS)
         with (
-            tc.tile_pool(name="tail", bufs=BLOCKS) as tail,
-            tc.psum_pool(name="tail_banks", bufs=BLOCKS) as tail_banks,
+            tc.tile_pool(name="tail", bufs=1) as tail,
+            tc.psum_pool(name="tail_banks", bufs=1) as tail_banks,
         ):
-            for b in range(BLOCKS):
-                neg_max = tail.tile([P, 1], F32, name="neg_max")
-                nc.vector.reduce_max(neg_max[:], scoreT[b][:], ALONG_ROW, negate=True)
-                expT = tail.tile([P, P], F32, name="expT")
-                exp_sum = tail.tile([P, 1], F32, name="exp_sum")
-                nc.scalar.activation(expT[:], scoreT[b][:], EXP, bias=neg_max[:, 0:1], accum_out=exp_sum[:, 0:1])
-                inv_sum = tail.tile([P, 1], F32, name="inv_sum")
-                nc.vector.reciprocal(inv_sum[:], exp_sum[:])
-                pT = tail.tile([P, P], BF16, name="pT")
-                nc.vector.tensor_scalar(pT[:], expT[:], inv_sum[:, 0:1], 1.0 / P, MULT, MULT)
+            neg_max = [tail.tile([P, 1], F32, name=f"neg_max{b}") for b in blocks]
+            exp_sum = [tail.tile([P, 1], F32, name=f"exp_sum{b}") for b in blocks]
+            inv_sum = [tail.tile([P, 1], F32, name=f"inv_sum{b}") for b in blocks]
+            expT = [tail.tile([P, P], F32, name=f"expT{b}") for b in blocks]
+            pT = [tail.tile([P, P], BF16, name=f"pT{b}") for b in blocks]
+            p_ps = [tail_banks.tile([P, P], BF16, name=f"p_ps{b}") for b in blocks]
+            p_sb = [tail.tile([P, P], BF16, name=f"p_sb{b}") for b in blocks]
+            out_ps = [tail_banks.tile([P, P], F32, name=f"out_ps{b}") for b in blocks]
+            out_sb = [tail.tile([P, P], F32, name=f"out_sb{b}") for b in blocks]
 
-                p_ps = tail_banks.tile([P, P], BF16, name="p_ps")
-                nc.tensor.transpose(p_ps[:], pT[:], identity[:])
-                p_sb = tail.tile([P, P], BF16, name="p_sb")
-                nc.vector.tensor_copy(p_sb[:], p_ps[:])
+            for b in blocks:
+                nc.vector.reduce_max(neg_max[b][:], scoreT[b][:], ALONG_ROW, negate=True)
+            for b in blocks:
+                nc.scalar.activation(
+                    expT[b][:], scoreT[b][:], EXP, bias=neg_max[b][:, 0:1], accum_out=exp_sum[b][:, 0:1]
+                )
+            for b in blocks:
+                nc.vector.reciprocal(inv_sum[b][:], exp_sum[b][:])
 
-                out_ps = tail_banks.tile([P, P], F32, name="out_ps")
-                nc.tensor.matmul(out_ps[:], imgT_sb[:], p_sb[:], start=True, stop=True)
-                out_sb = tail.tile([P, P], F32, name="out_sb")
-                nc.vector.tensor_copy(out_sb[:], out_ps[:])
-                nc.sync.dma_start(out[:, b * P : (b + 1) * P], out_sb[:])
+            nc.vector.tensor_scalar_mul(pT[0][:], expT[0][:], inv_sum[0][:, 0:1])
+            nc.scalar.mul(pT[1][:], expT[1][:], inv_sum[1][:, 0:1])
+            for b in blocks:
+                nc.tensor.transpose(p_ps[b][:], pT[b][:], identity[:])
+            nc.vector.tensor_copy(p_sb[0][:], p_ps[0][:])
+            nc.scalar.copy(p_sb[1][:], p_ps[1][:])
+            for b in blocks:
+                nc.tensor.matmul(out_ps[b][:], imgT_sb[:], p_sb[b][:], start=True, stop=True)
+            nc.vector.tensor_scalar_mul(out_sb[0][:], out_ps[0][:], 1.0 / P)
+            nc.scalar.mul(out_sb[1][:], out_ps[1][:], 1.0 / P)
+            nc.sync.dma_start(out[:, 0:P], out_sb[0][:])
+            nc.scalar.dma_start(out[:, P : 2 * P], out_sb[1][:])

@@ -5,6 +5,8 @@ P = 128
 S = 1024
 N = 256
 BLOCKS = N // P
+GROUP = 8
+EDGE = 8
 
 FLOPS = 2 * P * P * (N + P + N + N)
 BYTES = 2 * P * N + 3 * 2 * P * P + 4 * P + 2 * P + 2 * P * (N // 16) + 4 * P * N
@@ -19,6 +21,7 @@ def tile_imgwordatt_kernel(tc, table, w_aw, b_aw, img, w_ai, w_att, offs, out):
     with (
         tc.tile_pool(name="held", bufs=1) as held,
         tc.tile_pool(name="tanh_ring", bufs=4) as tanh_ring,
+        tc.tile_pool(name="group_ring", bufs=3) as group_ring,
         tc.psum_pool(name="score_banks", bufs=1) as score_banks,
     ):
         offsets = held.tile([P, N // 16], U16, name="offsets")
@@ -57,13 +60,33 @@ def tile_imgwordatt_kernel(tc, table, w_aw, b_aw, img, w_ai, w_att, offs, out):
             nc.vector.tensor_copy(imgT_sb[:], imgT_ps[:])
 
         scoreT = [score_banks.tile([P, P], F32, name=f"scoreT{b}") for b in range(BLOCKS)]
-        for r in range(P):
-            tanh_r = tanh_ring.tile([P, N], BF16, name="tanh_r")
-            nc.scalar.activation(tanh_r[:], aw_sb[:], TANH, bias=ai_sb[:, r : r + 1])
+
+        def sum_over_h(tanh_r, r):
             for b in range(BLOCKS):
                 nc.tensor.matmul(
                     scoreT[b][:, r : r + 1], tanh_r[:, b * P : (b + 1) * P], w_att_sb[:, 0:1], start=True, stop=True
                 )
+
+        def one_region(r):
+            tanh_r = tanh_ring.tile([P, N], BF16, name="tanh_r")
+            nc.scalar.activation(tanh_r[:], aw_sb[:], TANH, bias=ai_sb[:, r : r + 1])
+            sum_over_h(tanh_r, r)
+
+        def group_of_regions(first):
+            sums = group_ring.tile([P, GROUP * N], F32, name="sums")
+            for k in range(GROUP):
+                nc.vector.tensor_scalar_add(sums[:, k * N : (k + 1) * N], aw_sb[:], ai_sb[:, first + k : first + k + 1])
+            tanh_g = group_ring.tile([P, GROUP * N], BF16, name="tanh_g")
+            nc.scalar.activation(tanh_g[:], sums[:], TANH)
+            for k in range(GROUP):
+                sum_over_h(tanh_g[:, k * N : (k + 1) * N], first + k)
+
+        for r in range(EDGE):
+            one_region(r)
+        for first in range(EDGE, P - EDGE, GROUP):
+            group_of_regions(first)
+        for r in range(P - EDGE, P):
+            one_region(r)
 
         blocks = range(BLOCKS)
         with (

@@ -71,6 +71,7 @@ def tile_imgwordatt_kernel(tc, table, w_aw, b_aw, img, w_ai, w_att, offs, out):
             tanh_r = tanh_ring.tile([P, N], BF16, name="tanh_r")
             nc.scalar.activation(tanh_r[:], aw_sb[:], TANH, bias=ai_sb[:, r : r + 1])
             sum_over_h(tanh_r, r)
+            return tanh_r
 
         def group_of_regions(first):
             sums = group_ring.tile([P, GROUP * N], F32, name="sums")
@@ -85,8 +86,10 @@ def tile_imgwordatt_kernel(tc, table, w_aw, b_aw, img, w_ai, w_att, offs, out):
             one_region(r)
         for first in range(EDGE, P - EDGE, GROUP):
             group_of_regions(first)
+        unused_ps = score_banks.tile([P, N], F32, name="unused_ps")
         for r in range(P - EDGE, P):
-            one_region(r)
+            tanh_r = one_region(r)
+            nc.tensor.matmul(unused_ps[:], identity[:], tanh_r[:], start=True, stop=True)
 
         blocks = range(BLOCKS)
         with (

@@ -26,17 +26,17 @@ def tile_imgwordatt_kernel(tc, table, w_aw, b_aw, img, w_ai, w_att, offs, out):
     ):
         offsets = held.tile([P, N // 16], U16, name="offsets")
         nc.sync.dma_start(offsets[:], offs)
+        w_aw_sb = held.tile([P, P], BF16, name="w_aw_sb")
+        nc.scalar.dma_start(w_aw_sb[:], w_aw)
+        b_aw_sb = held.tile([P, 1], F32, name="b_aw_sb")
+        nc.sync.dma_start(b_aw_sb[:], b_aw)
         table_sb = held.tile([P, S], BF16, name="table_sb")
         nc.sync.dma_start(table_sb[:, : S // 2], table[:, : S // 2])
         nc.scalar.dma_start(table_sb[:, S // 2 :], table[:, S // 2 :])
-        w_aw_sb = held.tile([P, P], BF16, name="w_aw_sb")
-        nc.sync.dma_start(w_aw_sb[:], w_aw)
+        w_ai_sb = held.tile([P, P], BF16, name="w_ai_sb")
+        nc.sync.dma_start(w_ai_sb[:], w_ai)
         img_sb = held.tile([P, P], BF16, name="img_sb")
         nc.scalar.dma_start(img_sb[:], img)
-        w_ai_sb = held.tile([P, P], BF16, name="w_ai_sb")
-        nc.scalar.dma_start(w_ai_sb[:], w_ai)
-        b_aw_sb = held.tile([P, 1], F32, name="b_aw_sb")
-        nc.sync.dma_start(b_aw_sb[:], b_aw)
         w_att_sb = held.tile([P, 1], BF16, name="w_att_sb")
         nc.scalar.dma_start(w_att_sb[:], w_att)
 
@@ -71,7 +71,6 @@ def tile_imgwordatt_kernel(tc, table, w_aw, b_aw, img, w_ai, w_att, offs, out):
             tanh_r = tanh_ring.tile([P, N], BF16, name="tanh_r")
             nc.scalar.activation(tanh_r[:], aw_sb[:], TANH, bias=ai_sb[:, r : r + 1])
             sum_over_h(tanh_r, r)
-            return tanh_r
 
         def group_of_regions(first):
             sums = group_ring.tile([P, GROUP * N], F32, name="sums")
@@ -86,10 +85,8 @@ def tile_imgwordatt_kernel(tc, table, w_aw, b_aw, img, w_ai, w_att, offs, out):
             one_region(r)
         for first in range(EDGE, P - EDGE, GROUP):
             group_of_regions(first)
-        unused_ps = score_banks.tile([P, N], F32, name="unused_ps")
         for r in range(P - EDGE, P):
-            tanh_r = one_region(r)
-            nc.tensor.matmul(unused_ps[:], identity[:], tanh_r[:], start=True, stop=True)
+            one_region(r)
 
         blocks = range(BLOCKS)
         with (

@@ -27,18 +27,18 @@ def tile_imgwordatt_kernel(tc, table, w_aw, b_aw, img, w_ai, w_att, offs, out):
         offsets = held.tile([P, N // 16], U16, name="offsets")
         nc.sync.dma_start(offsets[:], offs)
         w_aw_sb = held.tile([P, P], BF16, name="w_aw_sb")
-        nc.scalar.dma_start(w_aw_sb[:], w_aw)
-        b_aw_sb = held.tile([P, 1], F32, name="b_aw_sb")
-        nc.sync.dma_start(b_aw_sb[:], b_aw)
+        nc.sync.dma_start(w_aw_sb[:], w_aw)
         table_sb = held.tile([P, S], BF16, name="table_sb")
         nc.sync.dma_start(table_sb[:, : S // 2], table[:, : S // 2])
-        nc.scalar.dma_start(table_sb[:, S // 2 :], table[:, S // 2 :])
+        nc.sync.dma_start(table_sb[:, S // 2 :], table[:, S // 2 :])
+        b_aw_sb = held.tile([P, 1], F32, name="b_aw_sb")
+        nc.sync.dma_start(b_aw_sb[:], b_aw)
         w_ai_sb = held.tile([P, P], BF16, name="w_ai_sb")
         nc.sync.dma_start(w_ai_sb[:], w_ai)
         img_sb = held.tile([P, P], BF16, name="img_sb")
-        nc.scalar.dma_start(img_sb[:], img)
+        nc.sync.dma_start(img_sb[:], img)
         w_att_sb = held.tile([P, 1], BF16, name="w_att_sb")
-        nc.scalar.dma_start(w_att_sb[:], w_att)
+        nc.sync.dma_start(w_att_sb[:], w_att)
 
         identity = held.tile([P, P], BF16, name="identity")
         make_identity(nc, identity[:])

@@ -1,15 +1,19 @@
 import concourse.mybir as mybir
 from concourse.masks import make_identity
 
-P = 128
+D = 128
+M = 128
+R = 128
 S = 1024
 N = 256
+P = 128
 BLOCKS = N // P
 GROUP = 8
 EDGE = 8
+assert BLOCKS == 2 and (R - 2 * EDGE) % GROUP == 0
 
-FLOPS = 2 * P * P * (N + P + N + N)
-BYTES = 2 * P * N + 3 * 2 * P * P + 4 * P + 2 * P + 2 * P * (N // 16) + 4 * P * N
+FLOPS = 2 * D * M * N + 2 * D * M * R + 2 * M * R * N + 2 * R * D * N
+BYTES = 2 * D * N + 2 * (D * M + D * M + D * R) + 4 * M + 2 * M + 2 * P * (N // 16) + 4 * D * N
 
 BF16, F32, U16 = mybir.dt.bfloat16, mybir.dt.float32, mybir.dt.uint16
 TANH, EXP = mybir.ActivationFunctionType.Tanh, mybir.ActivationFunctionType.Exp
@@ -18,6 +22,7 @@ ALONG_ROW = mybir.AxisListType.X
 
 def tile_imgwordatt_kernel(tc, table, w_aw, b_aw, img, w_ai, w_att, offs, out):
     nc = tc.nc
+    blocks = range(BLOCKS)
     with (
         tc.tile_pool(name="held", bufs=1) as held,
         tc.tile_pool(name="tanh_ring", bufs=4) as tanh_ring,
@@ -26,69 +31,70 @@ def tile_imgwordatt_kernel(tc, table, w_aw, b_aw, img, w_ai, w_att, offs, out):
     ):
         offsets = held.tile([P, N // 16], U16, name="offsets")
         nc.sync.dma_start(offsets[:], offs)
-        w_aw_sb = held.tile([P, P], BF16, name="w_aw_sb")
+        w_aw_sb = held.tile([D, M], BF16, name="w_aw_sb")
         nc.sync.dma_start(w_aw_sb[:], w_aw)
-        table_sb = held.tile([P, S], BF16, name="table_sb")
+        table_sb = held.tile([D, S], BF16, name="table_sb")
         nc.sync.dma_start(table_sb[:, : S // 2], table[:, : S // 2])
         nc.sync.dma_start(table_sb[:, S // 2 :], table[:, S // 2 :])
-        b_aw_sb = held.tile([P, 1], F32, name="b_aw_sb")
+        b_aw_sb = held.tile([M, 1], F32, name="b_aw_sb")
         nc.sync.dma_start(b_aw_sb[:], b_aw)
-        w_ai_sb = held.tile([P, P], BF16, name="w_ai_sb")
+        w_ai_sb = held.tile([D, M], BF16, name="w_ai_sb")
         nc.sync.dma_start(w_ai_sb[:], w_ai)
-        img_sb = held.tile([P, P], BF16, name="img_sb")
+        img_sb = held.tile([D, R], BF16, name="img_sb")
         nc.sync.dma_start(img_sb[:], img)
-        w_att_sb = held.tile([P, 1], BF16, name="w_att_sb")
+        w_att_sb = held.tile([M, 1], BF16, name="w_att_sb")
         nc.sync.dma_start(w_att_sb[:], w_att)
 
         identity = held.tile([P, P], BF16, name="identity")
         make_identity(nc, identity[:])
 
-        aw_sb = held.tile([P, N], F32, name="aw_sb")
-        ai_sb = held.tile([P, P], F32, name="ai_sb")
-        imgT_sb = held.tile([P, P], BF16, name="imgT_sb")
+        aw_sb = held.tile([M, N], F32, name="aw_sb")
+        ai_b_sb = held.tile([M, R], F32, name="ai_b_sb")
+        imgT_sb = held.tile([R, D], BF16, name="imgT_sb")
         with tc.psum_pool(name="head_banks", bufs=1) as head_banks:
-            aw_ps = head_banks.tile([P, N], F32, name="aw_ps")
+            aw_ps = head_banks.tile([M, N], F32, name="aw_ps")
             nc.tensor.matmul(aw_ps[:], w_aw_sb[:], table_sb[:].indirect(offsets[:]), start=True, stop=True)
             nc.vector.tensor_copy(aw_sb[:], aw_ps[:])
 
-            ai_ps = head_banks.tile([P, P], F32, name="ai_ps")
+            ai_ps = head_banks.tile([M, R], F32, name="ai_ps")
             nc.tensor.matmul(ai_ps[:], w_ai_sb[:], img_sb[:], start=True, stop=True)
-            nc.vector.tensor_scalar_add(ai_sb[:], ai_ps[:], b_aw_sb[:, 0:1])
+            nc.vector.tensor_scalar_add(ai_b_sb[:], ai_ps[:], b_aw_sb[:, 0:1])
 
-            imgT_ps = head_banks.tile([P, P], BF16, name="imgT_ps")
+            imgT_ps = head_banks.tile([R, D], BF16, name="imgT_ps")
             nc.tensor.transpose(imgT_ps[:], img_sb[:], identity[:])
             nc.vector.tensor_copy(imgT_sb[:], imgT_ps[:])
 
-        scoreT = [score_banks.tile([P, P], F32, name=f"scoreT{b}") for b in range(BLOCKS)]
+        scoreT = [score_banks.tile([P, R], F32, name=f"scoreT{b}") for b in blocks]
 
         def sum_over_h(tanh_r, r):
-            for b in range(BLOCKS):
+            for b in blocks:
                 nc.tensor.matmul(
                     scoreT[b][:, r : r + 1], tanh_r[:, b * P : (b + 1) * P], w_att_sb[:, 0:1], start=True, stop=True
                 )
 
         def one_region(r):
-            tanh_r = tanh_ring.tile([P, N], BF16, name="tanh_r")
-            nc.scalar.activation(tanh_r[:], aw_sb[:], TANH, bias=ai_sb[:, r : r + 1])
+            tanh_r = tanh_ring.tile([M, N], BF16, name="tanh_r")
+            nc.scalar.activation(tanh_r[:], aw_sb[:], TANH, bias=ai_b_sb[:, r : r + 1])
             sum_over_h(tanh_r, r)
 
         def group_of_regions(first):
-            sums = group_ring.tile([P, GROUP * N], F32, name="sums")
+            sums = group_ring.tile([M, GROUP * N], F32, name="sums")
             for k in range(GROUP):
-                nc.vector.tensor_scalar_add(sums[:, k * N : (k + 1) * N], aw_sb[:], ai_sb[:, first + k : first + k + 1])
-            tanh_g = group_ring.tile([P, GROUP * N], BF16, name="tanh_g")
+                nc.vector.tensor_scalar_add(
+                    sums[:, k * N : (k + 1) * N], aw_sb[:], ai_b_sb[:, first + k : first + k + 1]
+                )
+            tanh_g = group_ring.tile([M, GROUP * N], BF16, name="tanh_g")
             nc.scalar.activation(tanh_g[:], sums[:], TANH)
             for k in range(GROUP):
                 sum_over_h(tanh_g[:, k * N : (k + 1) * N], first + k)
 
         for r in range(EDGE):
             one_region(r)
-        for first in range(EDGE, P - EDGE, GROUP):
+        for first in range(EDGE, R - EDGE, GROUP):
             group_of_regions(first)
-        for r in range(P - EDGE, P):
+        for r in range(R - EDGE, R):
             one_region(r)
 
-        blocks = range(BLOCKS)
         with (
             tc.tile_pool(name="tail", bufs=1) as tail,
             tc.psum_pool(name="tail_banks", bufs=1) as tail_banks,
@@ -96,12 +102,12 @@ def tile_imgwordatt_kernel(tc, table, w_aw, b_aw, img, w_ai, w_att, offs, out):
             neg_max = [tail.tile([P, 1], F32, name=f"neg_max{b}") for b in blocks]
             exp_sum = [tail.tile([P, 1], F32, name=f"exp_sum{b}") for b in blocks]
             inv_sum = [tail.tile([P, 1], F32, name=f"inv_sum{b}") for b in blocks]
-            expT = [tail.tile([P, P], F32, name=f"expT{b}") for b in blocks]
-            pT = [tail.tile([P, P], BF16, name=f"pT{b}") for b in blocks]
-            p_ps = [tail_banks.tile([P, P], BF16, name=f"p_ps{b}") for b in blocks]
-            p_sb = [tail.tile([P, P], BF16, name=f"p_sb{b}") for b in blocks]
-            out_ps = [tail_banks.tile([P, P], F32, name=f"out_ps{b}") for b in blocks]
-            out_sb = [tail.tile([P, P], F32, name=f"out_sb{b}") for b in blocks]
+            expT = [tail.tile([P, R], F32, name=f"expT{b}") for b in blocks]
+            pT = [tail.tile([P, R], BF16, name=f"pT{b}") for b in blocks]
+            p_ps = [tail_banks.tile([R, P], BF16, name=f"p_ps{b}") for b in blocks]
+            p_sb = [tail.tile([R, P], BF16, name=f"p_sb{b}") for b in blocks]
+            out_ps = [tail_banks.tile([D, P], F32, name=f"out_ps{b}") for b in blocks]
+            out_sb = [tail.tile([D, P], F32, name=f"out_sb{b}") for b in blocks]
 
             for b in blocks:
                 nc.vector.reduce_max(neg_max[b][:], scoreT[b][:], ALONG_ROW, negate=True)
@@ -120,7 +126,7 @@ def tile_imgwordatt_kernel(tc, table, w_aw, b_aw, img, w_ai, w_att, offs, out):
             nc.scalar.copy(p_sb[1][:], p_ps[1][:])
             for b in blocks:
                 nc.tensor.matmul(out_ps[b][:], imgT_sb[:], p_sb[b][:], start=True, stop=True)
-            nc.vector.tensor_scalar_mul(out_sb[0][:], out_ps[0][:], 1.0 / P)
-            nc.scalar.mul(out_sb[1][:], out_ps[1][:], 1.0 / P)
+            nc.vector.tensor_scalar_mul(out_sb[0][:], out_ps[0][:], 1.0 / R)
+            nc.scalar.mul(out_sb[1][:], out_ps[1][:], 1.0 / R)
             nc.sync.dma_start(out[:, 0:P], out_sb[0][:])
             nc.scalar.dma_start(out[:, P : 2 * P], out_sb[1][:])

@@ -7,22 +7,20 @@ R = 128
 S = 1024
 N = 256
 P = 128
-BLOCKS = N // P
+HALVES = 2
 GROUP = 8
 EDGE = 8
-assert BLOCKS == 2 and (R - 2 * EDGE) % GROUP == 0
+assert (R - 2 * EDGE) % GROUP == 0 and N % HALVES == 0
 
 FLOPS = 2 * D * M * N + 2 * D * M * R + 2 * M * R * N + 2 * R * D * N
 BYTES = 2 * D * N + 2 * (D * M + D * M + D * R) + 4 * M + 2 * M + 2 * P * (N // 16) + 4 * D * N
 
 BF16, F32, U16 = mybir.dt.bfloat16, mybir.dt.float32, mybir.dt.uint16
 TANH, EXP = mybir.ActivationFunctionType.Tanh, mybir.ActivationFunctionType.Exp
-ALONG_ROW = mybir.AxisListType.X
 
 
 def tile_imgwordatt_kernel(tc, table, w_aw, b_aw, img, w_ai, w_att, offs, out):
     nc = tc.nc
-    blocks = range(BLOCKS)
     with (
         tc.tile_pool(name="held", bufs=1) as held,
         tc.tile_pool(name="tanh_ring", bufs=4) as tanh_ring,
@@ -42,8 +40,11 @@ def tile_imgwordatt_kernel(tc, table, w_aw, b_aw, img, w_ai, w_att, offs, out):
         nc.sync.dma_start(w_ai_sb[:], w_ai)
         img_sb = held.tile([D, R], BF16, name="img_sb")
         nc.sync.dma_start(img_sb[:], img)
-        w_att_sb = held.tile([M, 1], BF16, name="w_att_sb")
-        nc.sync.dma_start(w_att_sb[:], w_att)
+        w_att_slide = held.tile([M, 2 * R], BF16, name="w_att_slide")
+        nc.vector.memset(w_att_slide[:], 0.0)
+        nc.sync.dma_start(w_att_slide[:, R : R + 1], w_att)
+        all_r = held.tile([R, D], BF16, name="all_r")
+        nc.vector.memset(all_r[:], float(R))
 
         identity = held.tile([P, P], BF16, name="identity")
         make_identity(nc, identity[:])
@@ -64,18 +65,17 @@ def tile_imgwordatt_kernel(tc, table, w_aw, b_aw, img, w_ai, w_att, offs, out):
             nc.tensor.transpose(imgT_ps[:], img_sb[:], identity[:])
             nc.vector.tensor_copy(imgT_sb[:], imgT_ps[:])
 
-        scoreT = [score_banks.tile([P, R], F32, name=f"scoreT{b}") for b in blocks]
+        score_ps = score_banks.tile([R, N], F32, name="score_ps")
 
         def sum_over_h(tanh_r, r):
-            for b in blocks:
-                nc.tensor.matmul(
-                    scoreT[b][:, r : r + 1], tanh_r[:, b * P : (b + 1) * P], w_att_sb[:, 0:1], start=True, stop=True
-                )
+            nc.tensor.matmul(
+                score_ps[:], w_att_slide[:, R - r : 2 * R - r], tanh_r, start=(r == 0), stop=(r == R - 1)
+            )
 
         def one_region(r):
             tanh_r = tanh_ring.tile([M, N], BF16, name="tanh_r")
             nc.scalar.activation(tanh_r[:], aw_sb[:], TANH, bias=ai_b_sb[:, r : r + 1])
-            sum_over_h(tanh_r, r)
+            sum_over_h(tanh_r[:], r)
 
         def group_of_regions(first):
             sums = group_ring.tile([M, GROUP * N], F32, name="sums")
@@ -99,34 +99,16 @@ def tile_imgwordatt_kernel(tc, table, w_aw, b_aw, img, w_ai, w_att, offs, out):
             tc.tile_pool(name="tail", bufs=1) as tail,
             tc.psum_pool(name="tail_banks", bufs=1) as tail_banks,
         ):
-            neg_max = [tail.tile([P, 1], F32, name=f"neg_max{b}") for b in blocks]
-            exp_sum = [tail.tile([P, 1], F32, name=f"exp_sum{b}") for b in blocks]
-            inv_sum = [tail.tile([P, 1], F32, name=f"inv_sum{b}") for b in blocks]
-            expT = [tail.tile([P, R], F32, name=f"expT{b}") for b in blocks]
-            pT = [tail.tile([P, R], BF16, name=f"pT{b}") for b in blocks]
-            p_ps = [tail_banks.tile([R, P], BF16, name=f"p_ps{b}") for b in blocks]
-            p_sb = [tail.tile([R, P], BF16, name=f"p_sb{b}") for b in blocks]
-            out_ps = [tail_banks.tile([D, P], F32, name=f"out_ps{b}") for b in blocks]
-            out_sb = [tail.tile([D, P], F32, name=f"out_sb{b}") for b in blocks]
-
-            for b in blocks:
-                nc.vector.reduce_max(neg_max[b][:], scoreT[b][:], ALONG_ROW, negate=True)
-            for b in blocks:
-                nc.scalar.activation(
-                    expT[b][:], scoreT[b][:], EXP, bias=neg_max[b][:, 0:1], accum_out=exp_sum[b][:, 0:1]
-                )
-            for b in blocks:
-                nc.vector.reciprocal(inv_sum[b][:], exp_sum[b][:])
-
-            nc.vector.tensor_scalar_mul(pT[0][:], expT[0][:], inv_sum[0][:, 0:1])
-            nc.scalar.mul(pT[1][:], expT[1][:], inv_sum[1][:, 0:1])
-            for b in blocks:
-                nc.tensor.transpose(p_ps[b][:], pT[b][:], identity[:])
-            nc.vector.tensor_copy(p_sb[0][:], p_ps[0][:])
-            nc.scalar.copy(p_sb[1][:], p_ps[1][:])
-            for b in blocks:
-                nc.tensor.matmul(out_ps[b][:], imgT_sb[:], p_sb[b][:], start=True, stop=True)
-            nc.vector.tensor_scalar_mul(out_sb[0][:], out_ps[0][:], 1.0 / R)
-            nc.scalar.mul(out_sb[1][:], out_ps[1][:], 1.0 / R)
-            nc.sync.dma_start(out[:, 0:P], out_sb[0][:])
-            nc.scalar.dma_start(out[:, P : 2 * P], out_sb[1][:])
+            exp_sb = tail.tile([R, N], BF16, name="exp_sb")
+            nc.scalar.activation(exp_sb[:], score_ps[:], EXP)
+            sum_ps = tail_banks.tile([D, N], F32, name="sum_ps")
+            nc.tensor.matmul(sum_ps[:], all_r[:], exp_sb[:], start=True, stop=True)
+            out_ps = tail_banks.tile([D, N], F32, name="out_ps")
+            nc.tensor.matmul(out_ps[:], imgT_sb[:], exp_sb[:], start=True, stop=True)
+            inv_sum = tail.tile([D, N], F32, name="inv_sum")
+            out_sb = tail.tile([D, N], F32, name="out_sb")
+            for half in range(HALVES):
+                cols = slice(half * (N // HALVES), (half + 1) * (N // HALVES))
+                nc.vector.reciprocal(inv_sum[:, cols], sum_ps[:, cols])
+                nc.vector.tensor_mul(out_sb[:, cols], out_ps[:, cols], inv_sum[:, cols])
+                nc.sync.dma_start(out[:, cols], out_sb[:, cols])

@@ -7,10 +7,13 @@ R = 128
 S = 1024
 N = 256
 P = 128
-HALVES = 2
+BLOCK = 128
+BLOCKS = N // BLOCK
+LAST = 16
 GROUP = 8
 EDGE = 8
-assert (R - 2 * EDGE) % GROUP == 0 and N % HALVES == 0
+AHEAD = 2
+assert N % BLOCK == 0 and BLOCK % 32 == 0 and (R - LAST - EDGE) % GROUP == 0 and EDGE <= LAST <= GROUP * BLOCKS
 
 FLOPS = 2 * D * M * N + 2 * D * M * R + 2 * M * R * N + 2 * R * D * N
 BYTES = 2 * D * N + 2 * (D * M + D * M + D * R) + 4 * M + 2 * M + 2 * P * (N // 16) + 4 * D * N
@@ -24,8 +27,9 @@ def tile_imgwordatt_kernel(tc, table, w_aw, b_aw, img, w_ai, w_att, offs, out):
     with (
         tc.tile_pool(name="held", bufs=1) as held,
         tc.tile_pool(name="tanh_ring", bufs=4) as tanh_ring,
-        tc.tile_pool(name="group_ring", bufs=3) as group_ring,
-        tc.psum_pool(name="score_banks", bufs=1) as score_banks,
+        tc.tile_pool(name="sums_ring", bufs=AHEAD + 1) as sums_ring,
+        tc.tile_pool(name="per_block", bufs=BLOCKS) as per_block,
+        tc.psum_pool(name="banks", bufs=1) as banks,
     ):
         offsets = held.tile([P, N // 16], U16, name="offsets")
         nc.sync.dma_start(offsets[:], offs)
@@ -49,66 +53,94 @@ def tile_imgwordatt_kernel(tc, table, w_aw, b_aw, img, w_ai, w_att, offs, out):
         identity = held.tile([P, P], BF16, name="identity")
         make_identity(nc, identity[:])
 
-        aw_sb = held.tile([M, N], F32, name="aw_sb")
+        def words(b):
+            return slice(b * BLOCK, (b + 1) * BLOCK)
+
         ai_b_sb = held.tile([M, R], F32, name="ai_b_sb")
+        ai_ps = banks.tile([M, R], F32, name="ai_ps")
+        nc.tensor.matmul(ai_ps[:], w_ai_sb[:], img_sb[:], start=True, stop=True)
+        nc.vector.tensor_scalar_add(ai_b_sb[:], ai_ps[:], b_aw_sb[:, 0:1])
+
+        aw_ps = banks.tile([M, N], F32, name="aw_ps")
+        nc.tensor.matmul(aw_ps[:], w_aw_sb[:], table_sb[:].indirect(offsets[:]), start=True, stop=True)
+        aw_sb = held.tile([M, N], F32, name="aw_sb")
+        nc.vector.tensor_copy(aw_sb[:], aw_ps[:])
+
+        imgT_ps = banks.tile([R, D], BF16, name="imgT_ps")
+        nc.tensor.transpose(imgT_ps[:], img_sb[:], identity[:])
         imgT_sb = held.tile([R, D], BF16, name="imgT_sb")
-        with tc.psum_pool(name="head_banks", bufs=1) as head_banks:
-            aw_ps = head_banks.tile([M, N], F32, name="aw_ps")
-            nc.tensor.matmul(aw_ps[:], w_aw_sb[:], table_sb[:].indirect(offsets[:]), start=True, stop=True)
-            nc.vector.tensor_copy(aw_sb[:], aw_ps[:])
+        nc.vector.tensor_copy(imgT_sb[:], imgT_ps[:])
 
-            ai_ps = head_banks.tile([M, R], F32, name="ai_ps")
-            nc.tensor.matmul(ai_ps[:], w_ai_sb[:], img_sb[:], start=True, stop=True)
-            nc.vector.tensor_scalar_add(ai_b_sb[:], ai_ps[:], b_aw_sb[:, 0:1])
+        score_ps = [banks.tile([R, BLOCK], F32, name=f"score_ps{b}") for b in range(BLOCKS)]
 
-            imgT_ps = head_banks.tile([R, D], BF16, name="imgT_ps")
-            nc.tensor.transpose(imgT_ps[:], img_sb[:], identity[:])
-            nc.vector.tensor_copy(imgT_sb[:], imgT_ps[:])
-
-        score_ps = score_banks.tile([R, N], F32, name="score_ps")
-
-        def sum_over_h(tanh_r, r):
-            nc.tensor.matmul(
-                score_ps[:], w_att_slide[:, R - r : 2 * R - r], tanh_r, start=(r == 0), stop=(r == R - 1)
-            )
-
-        def one_region(r):
-            tanh_r = tanh_ring.tile([M, N], BF16, name="tanh_r")
-            nc.scalar.activation(tanh_r[:], aw_sb[:], TANH, bias=ai_b_sb[:, r : r + 1])
-            sum_over_h(tanh_r[:], r)
-
-        def group_of_regions(first):
-            sums = group_ring.tile([M, GROUP * N], F32, name="sums")
-            for k in range(GROUP):
-                nc.vector.tensor_scalar_add(
-                    sums[:, k * N : (k + 1) * N], aw_sb[:], ai_b_sb[:, first + k : first + k + 1]
+        def sum_over_h(tanh_tile, at, unit):
+            r, first_word, width = unit
+            for lo in range(0, width, BLOCK):
+                nc.tensor.matmul(
+                    score_ps[(first_word + lo) // BLOCK][:],
+                    w_att_slide[:, R - r : 2 * R - r],
+                    tanh_tile[:, at + lo : at + lo + BLOCK],
+                    start=(r == 0),
+                    stop=(r == R - 1),
                 )
-            tanh_g = group_ring.tile([M, GROUP * N], BF16, name="tanh_g")
-            nc.scalar.activation(tanh_g[:], sums[:], TANH)
-            for k in range(GROUP):
-                sum_over_h(tanh_g[:, k * N : (k + 1) * N], first + k)
 
-        for r in range(EDGE):
-            one_region(r)
-        for first in range(EDGE, R - EDGE, GROUP):
-            group_of_regions(first)
-        for r in range(R - EDGE, R):
-            one_region(r)
+        def one_unit(unit):
+            r, first_word, width = unit
+            tanh_u = tanh_ring.tile([M, width], BF16, name=f"tanh_u{width}")
+            nc.scalar.activation(
+                tanh_u[:], aw_sb[:, first_word : first_word + width], TANH, bias=ai_b_sb[:, r : r + 1]
+            )
+            sum_over_h(tanh_u, 0, unit)
 
-        with (
-            tc.tile_pool(name="tail", bufs=1) as tail,
-            tc.psum_pool(name="tail_banks", bufs=1) as tail_banks,
-        ):
-            exp_sb = tail.tile([R, N], BF16, name="exp_sb")
-            nc.scalar.activation(exp_sb[:], score_ps[:], EXP)
-            sum_ps = tail_banks.tile([D, N], F32, name="sum_ps")
+        def add_group(group):
+            sums = sums_ring.tile([M, GROUP * N], F32, name="sums")
+            at = 0
+            for r, first_word, width in group:
+                nc.vector.tensor_scalar_add(
+                    sums[:, at : at + width], aw_sb[:, first_word : first_word + width], ai_b_sb[:, r : r + 1]
+                )
+                at += width
+            return sums
+
+        def tanh_group(group, sums):
+            size = sum(width for r, first_word, width in group)
+            tanh_g = tanh_ring.tile([M, GROUP * N], BF16, name="tanh_g")
+            nc.scalar.activation(tanh_g[:, :size], sums[:, :size], TANH)
+            at = 0
+            for unit in group:
+                sum_over_h(tanh_g, at, unit)
+                at += unit[2]
+
+        def finish(b):
+            exp_sb = per_block.tile([R, BLOCK], BF16, name="exp_sb")
+            nc.scalar.activation(exp_sb[:], score_ps[b][:], EXP)
+            sum_ps = banks.tile([D, BLOCK], F32, name="sum_ps")
             nc.tensor.matmul(sum_ps[:], all_r[:], exp_sb[:], start=True, stop=True)
-            out_ps = tail_banks.tile([D, N], F32, name="out_ps")
+            out_ps = banks.tile([D, BLOCK], F32, name="out_ps")
             nc.tensor.matmul(out_ps[:], imgT_sb[:], exp_sb[:], start=True, stop=True)
-            inv_sum = tail.tile([D, N], F32, name="inv_sum")
-            out_sb = tail.tile([D, N], F32, name="out_sb")
-            for half in range(HALVES):
-                cols = slice(half * (N // HALVES), (half + 1) * (N // HALVES))
-                nc.vector.reciprocal(inv_sum[:, cols], sum_ps[:, cols])
-                nc.vector.tensor_mul(out_sb[:, cols], out_ps[:, cols], inv_sum[:, cols])
-                nc.sync.dma_start(out[:, cols], out_sb[:, cols])
+            inv_sum = per_block.tile([D, BLOCK], F32, name="inv_sum")
+            nc.vector.reciprocal(inv_sum[:], sum_ps[:])
+            out_sb = per_block.tile([D, BLOCK], F32, name="out_sb")
+            nc.vector.tensor_mul(out_sb[:], out_ps[:], inv_sum[:])
+            nc.sync.dma_start(out[:, words(b)], out_sb[:])
+
+        first_units = [(r, 0, N) for r in range(EDGE)]
+        groups = [[(r, 0, N) for r in range(first, first + GROUP)] for first in range(EDGE, R - LAST, GROUP)]
+        for b in range(BLOCKS):
+            end = R - EDGE if b == BLOCKS - 1 else R
+            groups.append([(r, b * BLOCK, BLOCK) for r in range(R - LAST, end)])
+        last_units = [(r, N - BLOCK, BLOCK) for r in range(R - EDGE, R)]
+
+        ready = [add_group(group) for group in groups[:AHEAD]]
+        for unit in first_units:
+            one_unit(unit)
+        for i, group in enumerate(groups):
+            if i + AHEAD < len(groups):
+                ready.append(add_group(groups[i + AHEAD]))
+            tanh_group(group, ready[i])
+            for b in range(BLOCKS - 1):
+                if i > 0 and (R - 1, b * BLOCK, BLOCK) in groups[i - 1]:
+                    finish(b)
+        for unit in last_units:
+            one_unit(unit)
+        finish(BLOCKS - 1)

@@ -7,7 +7,7 @@ R = 128
 S = 1024
 N = 256
 P = 128
-BLOCK = 128
+BLOCK = 64
 BLOCKS = N // BLOCK
 LAST = 16
 GROUP = 8
@@ -29,15 +29,15 @@ def tile_imgwordatt_kernel(tc, table, w_aw, b_aw, img, w_ai, w_att, offs, out):
         tc.tile_pool(name="tanh_ring", bufs=4) as tanh_ring,
         tc.tile_pool(name="sums_ring", bufs=AHEAD + 1) as sums_ring,
         tc.tile_pool(name="per_block", bufs=BLOCKS) as per_block,
-        tc.psum_pool(name="banks", bufs=1) as banks,
+        tc.psum_pool(name="score_banks", bufs=1) as score_banks,
     ):
+        table_sb = held.tile([D, S], BF16, name="table_sb")
+        nc.sync.dma_start(table_sb[:, : S // 2], table[:, : S // 2])
+        nc.sync.dma_start(table_sb[:, S // 2 :], table[:, S // 2 :])
         offsets = held.tile([P, N // 16], U16, name="offsets")
         nc.sync.dma_start(offsets[:], offs)
         w_aw_sb = held.tile([D, M], BF16, name="w_aw_sb")
         nc.sync.dma_start(w_aw_sb[:], w_aw)
-        table_sb = held.tile([D, S], BF16, name="table_sb")
-        nc.sync.dma_start(table_sb[:, : S // 2], table[:, : S // 2])
-        nc.sync.dma_start(table_sb[:, S // 2 :], table[:, S // 2 :])
         b_aw_sb = held.tile([M, 1], F32, name="b_aw_sb")
         nc.sync.dma_start(b_aw_sb[:], b_aw)
         w_ai_sb = held.tile([D, M], BF16, name="w_ai_sb")
@@ -57,21 +57,22 @@ def tile_imgwordatt_kernel(tc, table, w_aw, b_aw, img, w_ai, w_att, offs, out):
             return slice(b * BLOCK, (b + 1) * BLOCK)
 
         ai_b_sb = held.tile([M, R], F32, name="ai_b_sb")
-        ai_ps = banks.tile([M, R], F32, name="ai_ps")
-        nc.tensor.matmul(ai_ps[:], w_ai_sb[:], img_sb[:], start=True, stop=True)
-        nc.vector.tensor_scalar_add(ai_b_sb[:], ai_ps[:], b_aw_sb[:, 0:1])
-
-        aw_ps = banks.tile([M, N], F32, name="aw_ps")
-        nc.tensor.matmul(aw_ps[:], w_aw_sb[:], table_sb[:].indirect(offsets[:]), start=True, stop=True)
         aw_sb = held.tile([M, N], F32, name="aw_sb")
-        nc.vector.tensor_copy(aw_sb[:], aw_ps[:])
-
-        imgT_ps = banks.tile([R, D], BF16, name="imgT_ps")
-        nc.tensor.transpose(imgT_ps[:], img_sb[:], identity[:])
         imgT_sb = held.tile([R, D], BF16, name="imgT_sb")
-        nc.vector.tensor_copy(imgT_sb[:], imgT_ps[:])
+        with tc.psum_pool(name="head_banks", bufs=1) as head_banks:
+            ai_ps = head_banks.tile([M, R], F32, name="ai_ps")
+            nc.tensor.matmul(ai_ps[:], w_ai_sb[:], img_sb[:], start=True, stop=True)
+            nc.vector.tensor_scalar_add(ai_b_sb[:], ai_ps[:], b_aw_sb[:, 0:1])
 
-        score_ps = [banks.tile([R, BLOCK], F32, name=f"score_ps{b}") for b in range(BLOCKS)]
+            aw_ps = head_banks.tile([M, N], F32, name="aw_ps")
+            nc.tensor.matmul(aw_ps[:], w_aw_sb[:], table_sb[:].indirect(offsets[:]), start=True, stop=True)
+            nc.vector.tensor_copy(aw_sb[:], aw_ps[:])
+
+            imgT_ps = head_banks.tile([R, D], BF16, name="imgT_ps")
+            nc.tensor.transpose(imgT_ps[:], img_sb[:], identity[:])
+            nc.vector.tensor_copy(imgT_sb[:], imgT_ps[:])
+
+        score_ps = [score_banks.tile([R, BLOCK], F32, name=f"score_ps{b}") for b in range(BLOCKS)]
 
         def sum_over_h(tanh_tile, at, unit):
             r, first_word, width = unit
@@ -111,12 +112,12 @@ def tile_imgwordatt_kernel(tc, table, w_aw, b_aw, img, w_ai, w_att, offs, out):
                 sum_over_h(tanh_g, at, unit)
                 at += unit[2]
 
-        def finish(b):
+        def finish(b, tail_banks):
             exp_sb = per_block.tile([R, BLOCK], BF16, name="exp_sb")
             nc.scalar.activation(exp_sb[:], score_ps[b][:], EXP)
-            sum_ps = banks.tile([D, BLOCK], F32, name="sum_ps")
+            sum_ps = tail_banks.tile([D, BLOCK], F32, name="sum_ps")
             nc.tensor.matmul(sum_ps[:], all_r[:], exp_sb[:], start=True, stop=True)
-            out_ps = banks.tile([D, BLOCK], F32, name="out_ps")
+            out_ps = tail_banks.tile([D, BLOCK], F32, name="out_ps")
             nc.tensor.matmul(out_ps[:], imgT_sb[:], exp_sb[:], start=True, stop=True)
             inv_sum = per_block.tile([D, BLOCK], F32, name="inv_sum")
             nc.vector.reciprocal(inv_sum[:], sum_ps[:])
@@ -131,16 +132,17 @@ def tile_imgwordatt_kernel(tc, table, w_aw, b_aw, img, w_ai, w_att, offs, out):
             groups.append([(r, b * BLOCK, BLOCK) for r in range(R - LAST, end)])
         last_units = [(r, N - BLOCK, BLOCK) for r in range(R - EDGE, R)]
 
-        ready = [add_group(group) for group in groups[:AHEAD]]
-        for unit in first_units:
-            one_unit(unit)
-        for i, group in enumerate(groups):
-            if i + AHEAD < len(groups):
-                ready.append(add_group(groups[i + AHEAD]))
-            tanh_group(group, ready[i])
-            for b in range(BLOCKS - 1):
-                if i > 0 and (R - 1, b * BLOCK, BLOCK) in groups[i - 1]:
-                    finish(b)
-        for unit in last_units:
-            one_unit(unit)
-        finish(BLOCKS - 1)
+        with tc.psum_pool(name="tail_banks", bufs=2) as tail_banks:
+            ready = [add_group(group) for group in groups[:AHEAD]]
+            for unit in first_units:
+                one_unit(unit)
+            for i, group in enumerate(groups):
+                if i + AHEAD < len(groups):
+                    ready.append(add_group(groups[i + AHEAD]))
+                tanh_group(group, ready[i])
+                for b in range(BLOCKS - 1):
+                    if i > 0 and (R - 1, b * BLOCK, BLOCK) in groups[i - 1]:
+                        finish(b, tail_banks)
+            for unit in last_units:
+                one_unit(unit)
+            finish(BLOCKS - 1, tail_banks)

@@ -12,7 +12,7 @@ BLOCKS = N // BLOCK
 LAST = 16
 GROUP = 8
 EDGE = 8
-AHEAD = 2
+AHEAD = 3
 assert N % BLOCK == 0 and BLOCK % 32 == 0 and (R - LAST - EDGE) % GROUP == 0 and EDGE <= LAST <= GROUP * BLOCKS
 
 FLOPS = 2 * D * M * N + 2 * D * M * R + 2 * M * R * N + 2 * R * D * N
@@ -26,7 +26,7 @@ def tile_imgwordatt_kernel(tc, table, w_aw, b_aw, img, w_ai, w_att, offs, out):
     nc = tc.nc
     with (
         tc.tile_pool(name="held", bufs=1) as held,
-        tc.tile_pool(name="tanh_ring", bufs=4) as tanh_ring,
+        tc.tile_pool(name="tanh_ring", bufs=8) as tanh_ring,
         tc.tile_pool(name="sums_ring", bufs=AHEAD + 1) as sums_ring,
         tc.tile_pool(name="per_block", bufs=BLOCKS) as per_block,
         tc.psum_pool(name="score_banks", bufs=1) as score_banks,

@@ -7,13 +7,11 @@ R = 128
 S = 1024
 N = 256
 P = 128
-BLOCK = 64
-BLOCKS = N // BLOCK
-LAST = 16
-GROUP = 8
+WIDTHS = (192, 64)
+GROUP_VALUES = 2048
 EDGE = 8
 AHEAD = 3
-assert N % BLOCK == 0 and BLOCK % 32 == 0 and (R - LAST - EDGE) % GROUP == 0 and EDGE <= LAST <= GROUP * BLOCKS
+assert sum(WIDTHS) == N and EDGE < R
 
 FLOPS = 2 * D * M * N + 2 * D * M * R + 2 * M * R * N + 2 * R * D * N
 BYTES = 2 * D * N + 2 * (D * M + D * M + D * R) + 4 * M + 2 * M + 2 * P * (N // 16) + 4 * D * N
@@ -24,11 +22,12 @@ TANH, EXP = mybir.ActivationFunctionType.Tanh, mybir.ActivationFunctionType.Exp
 
 def tile_imgwordatt_kernel(tc, table, w_aw, b_aw, img, w_ai, w_att, offs, out):
     nc = tc.nc
+    blocks = range(len(WIDTHS))
     with (
         tc.tile_pool(name="held", bufs=1) as held,
-        tc.tile_pool(name="tanh_ring", bufs=8) as tanh_ring,
+        tc.tile_pool(name="tanh_ring", bufs=EDGE) as tanh_ring,
         tc.tile_pool(name="sums_ring", bufs=AHEAD + 1) as sums_ring,
-        tc.tile_pool(name="per_block", bufs=BLOCKS) as per_block,
+        tc.tile_pool(name="per_block", bufs=1) as per_block,
         tc.psum_pool(name="score_banks", bufs=1) as score_banks,
     ):
         table_sb = held.tile([D, S], BF16, name="table_sb")
@@ -54,7 +53,7 @@ def tile_imgwordatt_kernel(tc, table, w_aw, b_aw, img, w_ai, w_att, offs, out):
         make_identity(nc, identity[:])
 
         def words(b):
-            return slice(b * BLOCK, (b + 1) * BLOCK)
+            return slice(sum(WIDTHS[:b]), sum(WIDTHS[: b + 1]))
 
         ai_b_sb = held.tile([M, R], F32, name="ai_b_sb")
         aw_sb = held.tile([M, N], F32, name="aw_sb")
@@ -72,77 +71,65 @@ def tile_imgwordatt_kernel(tc, table, w_aw, b_aw, img, w_ai, w_att, offs, out):
             nc.tensor.transpose(imgT_ps[:], img_sb[:], identity[:])
             nc.vector.tensor_copy(imgT_sb[:], imgT_ps[:])
 
-        score_ps = [score_banks.tile([R, BLOCK], F32, name=f"score_ps{b}") for b in range(BLOCKS)]
+        score_ps = [score_banks.tile([R, WIDTHS[b]], F32, name=f"score_ps{b}") for b in blocks]
 
-        def sum_over_h(tanh_tile, at, unit):
-            r, first_word, width = unit
-            for lo in range(0, width, BLOCK):
-                nc.tensor.matmul(
-                    score_ps[(first_word + lo) // BLOCK][:],
-                    w_att_slide[:, R - r : 2 * R - r],
-                    tanh_tile[:, at + lo : at + lo + BLOCK],
-                    start=(r == 0),
-                    stop=(r == R - 1),
-                )
-
-        def one_unit(unit):
-            r, first_word, width = unit
-            tanh_u = tanh_ring.tile([M, width], BF16, name=f"tanh_u{width}")
-            nc.scalar.activation(
-                tanh_u[:], aw_sb[:, first_word : first_word + width], TANH, bias=ai_b_sb[:, r : r + 1]
+        def sum_over_h(b, r, tanh_br):
+            nc.tensor.matmul(
+                score_ps[b][:], w_att_slide[:, R - r : 2 * R - r], tanh_br, start=(r == 0), stop=(r == R - 1)
             )
-            sum_over_h(tanh_u, 0, unit)
+
+        def one_unit(b, r):
+            tanh_u = tanh_ring.tile([M, WIDTHS[b]], BF16, name=f"tanh_u{b}")
+            nc.scalar.activation(tanh_u[:], aw_sb[:, words(b)], TANH, bias=ai_b_sb[:, r : r + 1])
+            sum_over_h(b, r, tanh_u[:])
 
         def add_group(group):
-            sums = sums_ring.tile([M, GROUP * N], F32, name="sums")
-            at = 0
-            for r, first_word, width in group:
+            sums = sums_ring.tile([M, GROUP_VALUES], F32, name="sums")
+            for k, (b, r) in enumerate(group):
                 nc.vector.tensor_scalar_add(
-                    sums[:, at : at + width], aw_sb[:, first_word : first_word + width], ai_b_sb[:, r : r + 1]
+                    sums[:, k * WIDTHS[b] : (k + 1) * WIDTHS[b]], aw_sb[:, words(b)], ai_b_sb[:, r : r + 1]
                 )
-                at += width
             return sums
 
         def tanh_group(group, sums):
-            size = sum(width for r, first_word, width in group)
-            tanh_g = tanh_ring.tile([M, GROUP * N], BF16, name="tanh_g")
-            nc.scalar.activation(tanh_g[:, :size], sums[:, :size], TANH)
-            at = 0
-            for unit in group:
-                sum_over_h(tanh_g, at, unit)
-                at += unit[2]
+            values = sum(WIDTHS[b] for b, r in group)
+            tanh_g = tanh_ring.tile([M, GROUP_VALUES], BF16, name="tanh_g")
+            nc.scalar.activation(tanh_g[:, :values], sums[:, :values], TANH)
+            for k, (b, r) in enumerate(group):
+                sum_over_h(b, r, tanh_g[:, k * WIDTHS[b] : (k + 1) * WIDTHS[b]])
 
         def finish(b, tail_banks):
-            exp_sb = per_block.tile([R, BLOCK], BF16, name="exp_sb")
+            exp_sb = per_block.tile([R, WIDTHS[b]], BF16, name=f"exp_sb{b}")
             nc.scalar.activation(exp_sb[:], score_ps[b][:], EXP)
-            sum_ps = tail_banks.tile([D, BLOCK], F32, name="sum_ps")
+            sum_ps = tail_banks.tile([D, WIDTHS[b]], F32, name=f"sum_ps{b}")
             nc.tensor.matmul(sum_ps[:], all_r[:], exp_sb[:], start=True, stop=True)
-            out_ps = tail_banks.tile([D, BLOCK], F32, name="out_ps")
+            out_ps = tail_banks.tile([D, WIDTHS[b]], F32, name=f"out_ps{b}")
             nc.tensor.matmul(out_ps[:], imgT_sb[:], exp_sb[:], start=True, stop=True)
-            inv_sum = per_block.tile([D, BLOCK], F32, name="inv_sum")
+            inv_sum = per_block.tile([D, WIDTHS[b]], F32, name=f"inv_sum{b}")
             nc.vector.reciprocal(inv_sum[:], sum_ps[:])
-            out_sb = per_block.tile([D, BLOCK], F32, name="out_sb")
+            out_sb = per_block.tile([D, WIDTHS[b]], F32, name=f"out_sb{b}")
             nc.vector.tensor_mul(out_sb[:], out_ps[:], inv_sum[:])
             nc.sync.dma_start(out[:, words(b)], out_sb[:])
 
-        first_units = [(r, 0, N) for r in range(EDGE)]
-        groups = [[(r, 0, N) for r in range(first, first + GROUP)] for first in range(EDGE, R - LAST, GROUP)]
-        for b in range(BLOCKS):
-            end = R - EDGE if b == BLOCKS - 1 else R
-            groups.append([(r, b * BLOCK, BLOCK) for r in range(R - LAST, end)])
-        last_units = [(r, N - BLOCK, BLOCK) for r in range(R - EDGE, R)]
+        first_units = [(0, r) for r in range(EDGE)]
+        last_units = [(blocks[-1], r) for r in range(R - EDGE, R)]
+        groups = []
+        for b in blocks:
+            grouped = [(b, r) for r in range(R) if (b, r) not in first_units + last_units]
+            units_in_group = GROUP_VALUES // WIDTHS[b]
+            groups.extend(grouped[i : i + units_in_group] for i in range(0, len(grouped), units_in_group))
 
-        with tc.psum_pool(name="tail_banks", bufs=2) as tail_banks:
+        with tc.psum_pool(name="tail_banks", bufs=1) as tail_banks:
             ready = [add_group(group) for group in groups[:AHEAD]]
-            for unit in first_units:
-                one_unit(unit)
+            for b, r in first_units:
+                one_unit(b, r)
             for i, group in enumerate(groups):
                 if i + AHEAD < len(groups):
                     ready.append(add_group(groups[i + AHEAD]))
                 tanh_group(group, ready[i])
-                for b in range(BLOCKS - 1):
-                    if i > 0 and (R - 1, b * BLOCK, BLOCK) in groups[i - 1]:
+                for b in blocks[:-1]:
+                    if i > 0 and (b, R - 1) in groups[i - 1]:
                         finish(b, tail_banks)
-            for unit in last_units:
-                one_unit(unit)
-            finish(BLOCKS - 1, tail_banks)
+            for b, r in last_units:
+                one_unit(b, r)
+            finish(blocks[-1], tail_banks)

@@ -116,8 +116,12 @@ def tile_imgwordatt_kernel(tc, table, w_aw, b_aw, img, w_ai, w_att, offs, out):
         groups = []
         for b in blocks:
             grouped = [(b, r) for r in range(R) if (b, r) not in first_units + last_units]
-            units_in_group = GROUP_VALUES // WIDTHS[b]
-            groups.extend(grouped[i : i + units_in_group] for i in range(0, len(grouped), units_in_group))
+            block_groups, units_in_group = [], EDGE
+            while grouped:
+                block_groups.append(grouped[-units_in_group:])
+                grouped = grouped[:-units_in_group]
+                units_in_group = min(2 * units_in_group, GROUP_VALUES // WIDTHS[b])
+            groups.extend(reversed(block_groups))
 
         with tc.psum_pool(name="tail_banks", bufs=1) as tail_banks:
             ready = [add_group(group) for group in groups[:AHEAD]]

import concourse.mybir as mybir
from concourse.masks import make_identity

D = 128
M = 128
R = 128
S = 1024
N = 256
P = 128
WIDTHS = (192, 64)
GROUP_VALUES = 2048
EDGE = 8
AHEAD = 3
assert sum(WIDTHS) == N and EDGE < R

FLOPS = 2 * D * M * N + 2 * D * M * R + 2 * M * R * N + 2 * R * D * N
BYTES = 2 * D * N + 2 * (D * M + D * M + D * R) + 4 * M + 2 * M + 2 * P * (N // 16) + 4 * D * N

BF16, F32, U16 = mybir.dt.bfloat16, mybir.dt.float32, mybir.dt.uint16
TANH, EXP = mybir.ActivationFunctionType.Tanh, mybir.ActivationFunctionType.Exp


def tile_imgwordatt_kernel(tc, table, w_aw, b_aw, img, w_ai, w_att, offs, out):
    nc = tc.nc
    blocks = range(len(WIDTHS))
    with (
        tc.tile_pool(name="held", bufs=1) as held,
        tc.tile_pool(name="tanh_ring", bufs=EDGE) as tanh_ring,
        tc.tile_pool(name="sums_ring", bufs=AHEAD + 1) as sums_ring,
        tc.tile_pool(name="per_block", bufs=1) as per_block,
        tc.psum_pool(name="score_banks", bufs=1) as score_banks,
    ):
        table_sb = held.tile([D, S], BF16, name="table_sb")
        nc.sync.dma_start(table_sb[:, : S // 2], table[:, : S // 2])
        nc.sync.dma_start(table_sb[:, S // 2 :], table[:, S // 2 :])
        offsets = held.tile([P, N // 16], U16, name="offsets")
        nc.sync.dma_start(offsets[:], offs)
        w_aw_sb = held.tile([D, M], BF16, name="w_aw_sb")
        nc.sync.dma_start(w_aw_sb[:], w_aw)
        b_aw_sb = held.tile([M, 1], F32, name="b_aw_sb")
        nc.sync.dma_start(b_aw_sb[:], b_aw)
        w_ai_sb = held.tile([D, M], BF16, name="w_ai_sb")
        nc.sync.dma_start(w_ai_sb[:], w_ai)
        img_sb = held.tile([D, R], BF16, name="img_sb")
        nc.sync.dma_start(img_sb[:], img)
        w_att_slide = held.tile([M, 2 * R], BF16, name="w_att_slide")
        nc.vector.memset(w_att_slide[:], 0.0)
        nc.sync.dma_start(w_att_slide[:, R : R + 1], w_att)
        all_r = held.tile([R, D], BF16, name="all_r")
        nc.vector.memset(all_r[:], float(R))

        identity = held.tile([P, P], BF16, name="identity")
        make_identity(nc, identity[:])

        def words(b):
            return slice(sum(WIDTHS[:b]), sum(WIDTHS[: b + 1]))

        ai_b_sb = held.tile([M, R], F32, name="ai_b_sb")
        aw_sb = held.tile([M, N], F32, name="aw_sb")
        imgT_sb = held.tile([R, D], BF16, name="imgT_sb")
        with tc.psum_pool(name="head_banks", bufs=1) as head_banks:
            ai_ps = head_banks.tile([M, R], F32, name="ai_ps")
            nc.tensor.matmul(ai_ps[:], w_ai_sb[:], img_sb[:], start=True, stop=True)
            nc.vector.tensor_scalar_add(ai_b_sb[:], ai_ps[:], b_aw_sb[:, 0:1])

            aw_ps = head_banks.tile([M, N], F32, name="aw_ps")
            nc.tensor.matmul(aw_ps[:], w_aw_sb[:], table_sb[:].indirect(offsets[:]), start=True, stop=True)
            nc.vector.tensor_copy(aw_sb[:], aw_ps[:])

            imgT_ps = head_banks.tile([R, D], BF16, name="imgT_ps")
            nc.tensor.transpose(imgT_ps[:], img_sb[:], identity[:])
            nc.vector.tensor_copy(imgT_sb[:], imgT_ps[:])

        score_ps = [score_banks.tile([R, WIDTHS[b]], F32, name=f"score_ps{b}") for b in blocks]

        def sum_over_h(b, r, tanh_br):
            nc.tensor.matmul(
                score_ps[b][:], w_att_slide[:, R - r : 2 * R - r], tanh_br, start=(r == 0), stop=(r == R - 1)
            )

        def one_unit(b, r):
            tanh_u = tanh_ring.tile([M, WIDTHS[b]], BF16, name=f"tanh_u{b}")
            nc.scalar.activation(tanh_u[:], aw_sb[:, words(b)], TANH, bias=ai_b_sb[:, r : r + 1])
            sum_over_h(b, r, tanh_u[:])

        def add_group(group):
            sums = sums_ring.tile([M, GROUP_VALUES], F32, name="sums")
            for k, (b, r) in enumerate(group):
                nc.vector.tensor_scalar_add(
                    sums[:, k * WIDTHS[b] : (k + 1) * WIDTHS[b]], aw_sb[:, words(b)], ai_b_sb[:, r : r + 1]
                )
            return sums

        def tanh_group(group, sums):
            values = sum(WIDTHS[b] for b, r in group)
            tanh_g = tanh_ring.tile([M, GROUP_VALUES], BF16, name="tanh_g")
            nc.scalar.activation(tanh_g[:, :values], sums[:, :values], TANH)
            for k, (b, r) in enumerate(group):
                sum_over_h(b, r, tanh_g[:, k * WIDTHS[b] : (k + 1) * WIDTHS[b]])

        def finish(b, tail_banks):
            exp_sb = per_block.tile([R, WIDTHS[b]], BF16, name=f"exp_sb{b}")
            nc.scalar.activation(exp_sb[:], score_ps[b][:], EXP)
            sum_ps = tail_banks.tile([D, WIDTHS[b]], F32, name=f"sum_ps{b}")
            nc.tensor.matmul(sum_ps[:], all_r[:], exp_sb[:], start=True, stop=True)
            out_ps = tail_banks.tile([D, WIDTHS[b]], F32, name=f"out_ps{b}")
            nc.tensor.matmul(out_ps[:], imgT_sb[:], exp_sb[:], start=True, stop=True)
            inv_sum = per_block.tile([D, WIDTHS[b]], F32, name=f"inv_sum{b}")
            nc.vector.reciprocal(inv_sum[:], sum_ps[:])
            out_sb = per_block.tile([D, WIDTHS[b]], F32, name=f"out_sb{b}")
            nc.vector.tensor_mul(out_sb[:], out_ps[:], inv_sum[:])
            nc.sync.dma_start(out[:, words(b)], out_sb[:])

        first_units = [(0, r) for r in range(EDGE)]
        last_units = [(blocks[-1], r) for r in range(R - EDGE, R)]
        groups = []
        for b in blocks:
            grouped = [(b, r) for r in range(R) if (b, r) not in first_units + last_units]
            block_groups, units_in_group = [], EDGE
            while grouped:
                block_groups.append(grouped[-units_in_group:])
                grouped = grouped[:-units_in_group]
                units_in_group = min(2 * units_in_group, GROUP_VALUES // WIDTHS[b])
            groups.extend(reversed(block_groups))

        with tc.psum_pool(name="tail_banks", bufs=1) as tail_banks:
            ready = [add_group(group) for group in groups[:AHEAD]]
            for b, r in first_units:
                one_unit(b, r)
            for i, group in enumerate(groups):
                if i + AHEAD < len(groups):
                    ready.append(add_group(groups[i + AHEAD]))
                tanh_group(group, ready[i])
                for b in blocks[:-1]:
                    if i > 0 and (b, R - 1) in groups[i - 1]:
                        finish(b, tail_banks)
            for b, r in last_units:
                one_unit(b, r)
            finish(blocks[-1], tail_banks)
